import numpy as np
import ml_dtypes


def mxq(x, axis, fmt="e4m3"):
    dtype, down = {"e4m3": (ml_dtypes.float8_e4m3fn, 7), "e5m2": (ml_dtypes.float8_e5m2, 14)}[fmt]
    v = np.moveaxis(np.asarray(x, np.float32).astype(ml_dtypes.bfloat16).astype(np.float64), axis, -1)
    blocks = v.reshape(v.shape[:-1] + (-1, 32))
    amax = np.abs(blocks).max(-1, keepdims=True)
    byte = np.maximum(np.where(amax > 0, np.frexp(amax)[1] - 1 + 127, 0) - down, 1)
    scale = np.exp2(byte - 127.0)
    codes = (blocks / scale).astype(np.float32).astype(dtype).astype(np.float64)
    return np.moveaxis((codes * scale).reshape(v.shape), -1, axis)


WIDE = False


def mx_kscale(k):
    if not WIDE:
        return np.ones(k)
    levels = np.array([10, -10, 5, -5, 0])
    a = np.random.permutation(np.resize(levels, k // 512 * 4)).reshape(k // 512, 4)
    idx = np.arange(k)
    return np.exp2(a[idx // 512, idx % 128 // 32])


BF16 = ml_dtypes.bfloat16


def bf(x):
    return np.asarray(x, np.float32).astype(BF16)


def f64(x):
    return np.asarray(x).astype(np.float64)


E2M1 = np.array([0.0, 0.5, 1.0, 1.5, 2.0, 3.0, 4.0, 6.0, -0.0, -0.5, -1.0, -1.5, -2.0, -3.0, -4.0, -6.0])


def pack_weight(w, fmt):
    k, n = w.shape
    w = f64(bf(w)).reshape(k // 32, 32, n)
    amax = np.abs(w).max(1)
    if fmt == "e4m3":
        byte = np.frexp(amax)[1] - 1 + 127 - 7
    else:
        mant, ex = np.frexp(amax / 6.0)
        byte = np.where(mant > 0.5, ex, ex - 1) + 127
    byte = np.clip(np.where(amax > 0, byte, 1), 1, 254)
    scaled = (w * np.exp2(127.0 - byte)[:, None, :]).reshape(k, n).astype(np.float32)
    by_word = np.ascontiguousarray(scaled.reshape(k // 512, 128, 4, n).transpose(0, 1, 3, 2))
    if fmt == "e4m3":
        words = by_word.astype(ml_dtypes.float8_e4m3fn).view(np.uint8)
    else:
        c = by_word.astype(ml_dtypes.float4_e2m1fn).view(np.uint8) & 0xF
        words = c[..., 0::2] | (c[..., 1::2] << 4)
    return np.ascontiguousarray(words), np.ascontiguousarray(byte.astype(np.uint8).reshape(k // 512, 16, n))


def unpack_weight(words, scales, fmt):
    g, p, n, _ = words.shape
    if fmt == "e4m3":
        vals = np.ascontiguousarray(words).view(ml_dtypes.float8_e4m3fn).astype(np.float64)
    else:
        nib = np.empty((g, p, n, 4), np.uint8)
        nib[..., 0::2] = words & 0xF
        nib[..., 1::2] = words >> 4
        vals = E2M1[nib]
    vals = vals * np.repeat(np.exp2(scales.astype(np.float64) - 127.0), 8, axis=1)[..., None]
    return vals.transpose(0, 1, 3, 2).reshape(g * 512, n)


B, R, C, H, DH = 64, 8, 1024, 4, 128
T = R * R
E = H * DH
EPS = 2.0 ** -23
FMT = "e4m3"


def rmsnorm(v):
    return v * (1.0 / np.sqrt(np.mean(np.square(v), axis=-1, keepdims=True) + EPS))


def setup_inputs():
    s = mx_kscale(C)
    x = bf(np.random.standard_normal((B, T, C)) * s)
    Wq_words, Wq_scales = pack_weight(np.random.standard_normal((C, E)) / np.sqrt(C) / s[:, None], FMT)
    Wk_words, Wk_scales = pack_weight(np.random.standard_normal((C, E)) / np.sqrt(C) / s[:, None], FMT)
    return {"x": x,
            "Wq_words": Wq_words, "Wq_scales": Wq_scales,
            "Wk_words": Wk_words, "Wk_scales": Wk_scales}


def reference(x, Wq_words, Wq_scales, Wk_words, Wk_scales):
    xq = mxq(f64(x), 2, "e4m3")

    def proj(words, scales):
        return (xq @ unpack_weight(words, scales, FMT)).reshape(B, T, H, DH).transpose(0, 2, 1, 3)

    return rmsnorm(proj(Wq_words, Wq_scales)), rmsnorm(proj(Wk_words, Wk_scales))

@@ -1,0 +1,205 @@
+from contextlib import ExitStack
+
+import concourse.mybir as mybir
+from concourse.masks import make_identity
+
+F32 = mybir.dt.float32
+BF16 = mybir.dt.bfloat16
+I32 = mybir.dt.int32
+U32 = mybir.dt.uint32
+U8 = mybir.dt.uint8
+FP8X4 = mybir.dt.float8_e4m3fn_x4
+ACT = mybir.ActivationFunctionType
+ALU = mybir.AluOpType
+
+P = 128
+BOARDS = 64
+SQUARES = 64
+C = 1024
+HEADS = 4
+DH = 128
+E = HEADS * DH
+EPS = 2.0 ** -23
+
+PASSES = C // (4 * P)
+TILES = BOARDS * SQUARES // P
+HALVES = SQUARES // TILES
+RUN = 2
+RUNS = TILES // RUN
+STORE = 4
+
+FLOPS = 2 * BOARDS * SQUARES * C * 2 * E
+
+
+def tile_pieceroutedattention_pa_t_kernel(
+    tc, x, Wq_words, Wq_scales, Wk_words, Wk_scales, out_0, out_1
+):
+    nc = tc.nc
+    weights = ((Wq_words, Wq_scales), (Wk_words, Wk_scales))
+    outs = (out_0, out_1)
+    x_by_partition = x.rearrange("b (s j) c -> (b s) j c", s=HALVES)
+
+    with ExitStack() as stack:
+        stack.enter_context(tc.manual_schedule())
+        keep = stack.enter_context(tc.tile_pool(name="keep", bufs=1))
+        x_pool = stack.enter_context(tc.tile_pool(name="x", bufs=RUNS))
+        quant = stack.enter_context(tc.tile_pool(name="quant", bufs=3))
+        stats = stack.enter_context(tc.tile_pool(name="stats", bufs=4))
+        result = stack.enter_context(tc.tile_pool(name="result", bufs=3))
+        xt_psum = stack.enter_context(tc.psum_pool(name="xt_psum", bufs=RUN))
+        acc_psum = stack.enter_context(tc.psum_pool(name="acc_psum", bufs=8 - RUN))
+
+        w_planes = keep.tile([P, 2, PASSES, E], U8, align_bytes=64)
+        nc.vector.memset(w_planes[:].rearrange("p w g n -> p (w g n)").bitcast(I32), 0)
+        eps = keep.tile([P, 1], F32)
+        nc.vector.memset(eps[:], EPS)
+        warm = keep.tile([P, 1], F32)
+        nc.scalar.activation(out=warm[:], in_=eps[:], func=ACT.Sqrt)
+        ident = keep.tile([P, P], F32)
+        make_identity(nc, ident[:])
+        squares = keep.tile([P, DH], BF16)
+
+        x_tiles = []
+
+        def load_x(r):
+            x_run = x_pool.tile([P, RUN, C], BF16, name="x_run")
+            nc.sync.dma_start(out=x_run[:], in_=x_by_partition[:, RUN * r : RUN * (r + 1), :])
+            x_tiles.append(x_run)
+
+        load_x(0)
+        w_words = keep.tile([P, 2, PASSES, E], U32, align_bytes=64)
+        for w in range(2):
+            nc.sync.dma_start(
+                out=w_words[:, w, :, :].bitcast(I32),
+                in_=weights[w][0].rearrange("g p n t -> p g (n t)").bitcast(I32),
+            )
+        for w in range(2):
+            for quadrant in range(4):
+                nc.sync.dma_start(
+                    out=w_planes[32 * quadrant : 32 * quadrant + 4, w, :, :].bitcast(I32),
+                    in_=weights[w][1][:, 4 * quadrant : 4 * quadrant + 4, :]
+                    .rearrange("g r n -> r g n")
+                    .bitcast(I32),
+                )
+        for r in range(1, RUNS):
+            load_x(r)
+
+        xt_of = {}
+        grouped_of = {}
+        codes_of = {}
+        acc_of = {}
+        std_of = {}
+        out_of = {}
+
+        def transpose_run(r):
+            words = x_tiles[r][:].bitcast(F32)
+            for i in range(RUN):
+                xt = xt_psum.tile([P, 2 * PASSES, P], F32, name="xt")
+                for g in range(PASSES):
+                    for u in range(2):
+                        nc.tensor.transpose(
+                            xt[:, 2 * g + u, :],
+                            words[:, i, 256 * g + u : 256 * (g + 1) : 2],
+                            ident[:],
+                        )
+                xt_of[RUN * r + i] = xt
+            grouped_of[r] = quant.tile([P, RUN, PASSES, P, 4], BF16, name="grouped", align_bytes=64)
+
+        def copy_out(engine_copy, r, i):
+            engine_copy(
+                out=grouped_of[r][:, i, :, :, :]
+                .rearrange("p g n t -> p (g n t)")
+                .bitcast(F32)
+                .rearrange("p (g n u) -> p g n u", g=PASSES, u=2),
+                in_=xt_of[RUN * r + i][:].rearrange("p (g u) n -> p g n u", u=2),
+            )
+
+        def quantise_run(r):
+            codes = quant.tile([P, RUN, PASSES, P], U32, name="codes", align_bytes=64)
+            plane = quant.tile([P, RUN, PASSES, P], U8, name="plane", align_bytes=64)
+            nc.vector.quantize_mx(
+                out=codes[:].rearrange("p i g n -> p (i g n)").bitcast(FP8X4),
+                scales=plane[:].rearrange("p i g n -> p (i g n)"),
+                in_=grouped_of[r][:].rearrange("p i g n t -> p (i g n t)"),
+            )
+            codes_of[r] = (codes, plane)
+
+        def multiply_run(r):
+            codes, plane = codes_of[r]
+            for i in range(RUN):
+                acc = [acc_psum.tile([P, E], F32, name="acc") for w in range(2)]
+                for g in range(PASSES):
+                    for w in range(2):
+                        nc.tensor.matmul_mx(
+                            out=acc[w][:],
+                            lhsT=codes[:, i, g, :].bitcast(FP8X4),
+                            lhsT_scale=plane[:, i, g, :],
+                            rhs=w_words[:, w, g, :].bitcast(FP8X4),
+                            rhs_scale=w_planes[:, w, g, :],
+                            start=(g == 0),
+                            stop=(g == PASSES - 1),
+                        )
+                acc_of[RUN * r + i] = acc
+
+        def root_mean_square(j):
+            sums = stats.tile([P, 2 * HEADS], F32, name="sums")
+            for w in range(2):
+                for h in range(HEADS):
+                    nc.scalar.activation(
+                        out=squares[:],
+                        in_=acc_of[j][w][:, DH * h : DH * (h + 1)],
+                        func=ACT.Square,
+                        accum_out=sums[:, HEADS * w + h : HEADS * w + h + 1],
+                    )
+            std = stats.tile([P, 2 * HEADS], F32, name="std")
+            nc.scalar.activation(out=std[:], in_=sums[:], func=ACT.Sqrt, bias=eps[:], scale=1.0 / DH)
+            std_of[j] = std
+
+        def normalise(j):
+            group, place = divmod(j, STORE)
+            if place == 0:
+                out_of[group] = [
+                    result.tile([P, HEADS, STORE, DH], F32, name="normed%d" % w) for w in range(2)
+                ]
+            rstd = stats.tile([P, 2 * HEADS], F32, name="rstd")
+            nc.vector.reciprocal(rstd[:], std_of[j][:])
+            acc = acc_of[j]
+            for w in range(2):
+                nc.vector.tensor_tensor(
+                    out=out_of[group][w][:, :, place, :],
+                    in0=acc[w][:].rearrange("p (h d) -> p h d", h=HEADS),
+                    in1=rstd[:, HEADS * w : HEADS * (w + 1)].unsqueeze(2).to_broadcast([P, HEADS, DH]),
+                    op=ALU.mult,
+                )
+            if place == STORE - 1:
+                normed = out_of[group]
+                for w in range(2):
+                    for s in range(HALVES):
+                        first = TILES * s + STORE * group
+                        nc.sync.dma_start(
+                            out=outs[w][:, :, first : first + STORE, :].rearrange("b h j d -> b h (j d)"),
+                            in_=normed[w][s:P:HALVES, :, :, :].rearrange("p h j d -> p h (j d)"),
+                        )
+
+        for r in range(-1, RUNS + 1):
+            ahead = r + 1 < RUNS
+            here = 0 <= r < RUNS
+            behind = r >= 1
+            if ahead:
+                transpose_run(r + 1)
+            if behind:
+                normalise(RUN * (r - 1))
+            if ahead:
+                copy_out(nc.vector.tensor_copy, r + 1, 0)
+            if here:
+                multiply_run(r)
+            if behind:
+                root_mean_square(RUN * (r - 1) + 1)
+            if ahead:
+                copy_out(nc.scalar.copy, r + 1, 1)
+            if here:
+                root_mean_square(RUN * r)
+            if behind:
+                normalise(RUN * (r - 1) + 1)
+            if ahead:
+                quantise_run(r + 1)

@@ -24,9 +24,12 @@ EPS = 2.0 ** -23
 PASSES = C // (4 * P)
 TILES = BOARDS * SQUARES // P
 HALVES = SQUARES // TILES
-RUN = 2
-RUNS = TILES // RUN
+PAIR = 2
+PAIRS = TILES // PAIR
 STORE = 4
+LOOKAHEAD = 32
+VECTOR_COPIES_ONE_IN = 4
+PSUM_BANKS = 8
 
 FLOPS = 2 * BOARDS * SQUARES * C * 2 * E
 
@@ -42,12 +45,12 @@ def tile_pieceroutedattention_pa_t_kernel(
     with ExitStack() as stack:
         stack.enter_context(tc.manual_schedule())
         keep = stack.enter_context(tc.tile_pool(name="keep", bufs=1))
-        x_pool = stack.enter_context(tc.tile_pool(name="x", bufs=RUNS))
-        quant = stack.enter_context(tc.tile_pool(name="quant", bufs=3))
+        x_pool = stack.enter_context(tc.tile_pool(name="x", bufs=PAIRS))
+        stage = stack.enter_context(tc.tile_pool(name="stage", bufs=3))
+        mx_pool = stack.enter_context(tc.tile_pool(name="mx", bufs=PAIRS))
         stats = stack.enter_context(tc.tile_pool(name="stats", bufs=4))
         result = stack.enter_context(tc.tile_pool(name="result", bufs=3))
-        xt_psum = stack.enter_context(tc.psum_pool(name="xt_psum", bufs=RUN))
-        acc_psum = stack.enter_context(tc.psum_pool(name="acc_psum", bufs=8 - RUN))
+        banks = stack.enter_context(tc.psum_pool(name="banks", bufs=PSUM_BANKS))
 
         w_planes = keep.tile([P, 2, PASSES, E], U8, align_bytes=64)
         nc.vector.memset(w_planes[:].rearrange("p w g n -> p (w g n)").bitcast(I32), 0)
@@ -61,10 +64,12 @@ def tile_pieceroutedattention_pa_t_kernel(
 
         x_tiles = []
 
-        def load_x(r):
-            x_run = x_pool.tile([P, RUN, C], BF16, name="x_run")
-            nc.sync.dma_start(out=x_run[:], in_=x_by_partition[:, RUN * r : RUN * (r + 1), :])
-            x_tiles.append(x_run)
+        def load_x(pair):
+            x_pair = x_pool.tile([P, PAIR, C], BF16, name="x_pair")
+            nc.sync.dma_start(
+                out=x_pair[:], in_=x_by_partition[:, PAIR * pair : PAIR * (pair + 1), :]
+            )
+            x_tiles.append(x_pair)
 
         load_x(0)
         w_words = keep.tile([P, 2, PASSES, E], U32, align_bytes=64)
@@ -81,89 +86,80 @@ def tile_pieceroutedattention_pa_t_kernel(
                     .rearrange("g r n -> r g n")
                     .bitcast(I32),
                 )
-        for r in range(1, RUNS):
-            load_x(r)
+        for pair in range(1, PAIRS):
+            load_x(pair)
 
-        xt_of = {}
         grouped_of = {}
         codes_of = {}
-        acc_of = {}
-        std_of = {}
         out_of = {}
 
-        def transpose_run(r):
-            words = x_tiles[r][:].bitcast(F32)
-            for i in range(RUN):
-                xt = xt_psum.tile([P, 2 * PASSES, P], F32, name="xt")
-                for g in range(PASSES):
-                    for u in range(2):
-                        nc.tensor.transpose(
-                            xt[:, 2 * g + u, :],
-                            words[:, i, 256 * g + u : 256 * (g + 1) : 2],
-                            ident[:],
-                        )
-                xt_of[RUN * r + i] = xt
-            grouped_of[r] = quant.tile([P, RUN, PASSES, P, 4], BF16, name="grouped", align_bytes=64)
-
-        def copy_out(engine_copy, r, i):
-            engine_copy(
-                out=grouped_of[r][:, i, :, :, :]
+        def prepare(j):
+            pair, i = divmod(j, PAIR)
+            words = x_tiles[pair][:].bitcast(F32)
+            xt = banks.tile([P, 2 * PASSES, P], F32, name="xt", tag="bank")
+            for g in range(PASSES):
+                for u in range(2):
+                    nc.tensor.transpose(
+                        xt[:, 2 * g + u, :], words[:, i, 256 * g + u : 256 * (g + 1) : 2], ident[:]
+                    )
+            if i == 0:
+                grouped_of[pair] = stage.tile(
+                    [P, PAIR, PASSES, P, 4], BF16, name="grouped", align_bytes=64
+                )
+            copy_out = nc.vector.tensor_copy if j % VECTOR_COPIES_ONE_IN == 0 else nc.scalar.copy
+            copy_out(
+                out=grouped_of[pair][:, i, :, :, :]
                 .rearrange("p g n t -> p (g n t)")
                 .bitcast(F32)
                 .rearrange("p (g n u) -> p g n u", g=PASSES, u=2),
-                in_=xt_of[RUN * r + i][:].rearrange("p (g u) n -> p g n u", u=2),
+                in_=xt[:].rearrange("p (g u) n -> p g n u", u=2),
             )
+            if i == PAIR - 1:
+                codes = mx_pool.tile([P, PAIR, PASSES, P], U32, name="codes", align_bytes=64)
+                plane = mx_pool.tile([P, PAIR, PASSES, P], U8, name="plane", align_bytes=64)
+                nc.vector.quantize_mx(
+                    out=codes[:].rearrange("p i g n -> p (i g n)").bitcast(FP8X4),
+                    scales=plane[:].rearrange("p i g n -> p (i g n)"),
+                    in_=grouped_of[pair][:].rearrange("p i g n t -> p (i g n t)"),
+                )
+                codes_of[pair] = (codes, plane)
 
-        def quantise_run(r):
-            codes = quant.tile([P, RUN, PASSES, P], U32, name="codes", align_bytes=64)
-            plane = quant.tile([P, RUN, PASSES, P], U8, name="plane", align_bytes=64)
-            nc.vector.quantize_mx(
-                out=codes[:].rearrange("p i g n -> p (i g n)").bitcast(FP8X4),
-                scales=plane[:].rearrange("p i g n -> p (i g n)"),
-                in_=grouped_of[r][:].rearrange("p i g n t -> p (i g n t)"),
-            )
-            codes_of[r] = (codes, plane)
-
-        def multiply_run(r):
-            codes, plane = codes_of[r]
-            for i in range(RUN):
-                acc = [acc_psum.tile([P, E], F32, name="acc") for w in range(2)]
+        def project_and_normalise(j):
+            pair, i = divmod(j, PAIR)
+            codes, plane = codes_of[pair]
+            acc = []
+            for w in range(2):
+                acc.append(banks.tile([P, E], F32, name="acc", tag="bank"))
                 for g in range(PASSES):
-                    for w in range(2):
-                        nc.tensor.matmul_mx(
-                            out=acc[w][:],
-                            lhsT=codes[:, i, g, :].bitcast(FP8X4),
-                            lhsT_scale=plane[:, i, g, :],
-                            rhs=w_words[:, w, g, :].bitcast(FP8X4),
-                            rhs_scale=w_planes[:, w, g, :],
-                            start=(g == 0),
-                            stop=(g == PASSES - 1),
-                        )
-                acc_of[RUN * r + i] = acc
+                    nc.tensor.matmul_mx(
+                        out=acc[w][:],
+                        lhsT=codes[:, i, g, :].bitcast(FP8X4),
+                        lhsT_scale=plane[:, i, g, :],
+                        rhs=w_words[:, w, g, :].bitcast(FP8X4),
+                        rhs_scale=w_planes[:, w, g, :],
+                        start=(g == 0),
+                        stop=(g == PASSES - 1),
+                    )
 
-        def root_mean_square(j):
             sums = stats.tile([P, 2 * HEADS], F32, name="sums")
             for w in range(2):
                 for h in range(HEADS):
                     nc.scalar.activation(
                         out=squares[:],
-                        in_=acc_of[j][w][:, DH * h : DH * (h + 1)],
+                        in_=acc[w][:, DH * h : DH * (h + 1)],
                         func=ACT.Square,
                         accum_out=sums[:, HEADS * w + h : HEADS * w + h + 1],
                     )
             std = stats.tile([P, 2 * HEADS], F32, name="std")
             nc.scalar.activation(out=std[:], in_=sums[:], func=ACT.Sqrt, bias=eps[:], scale=1.0 / DH)
-            std_of[j] = std
 
-        def normalise(j):
             group, place = divmod(j, STORE)
             if place == 0:
                 out_of[group] = [
                     result.tile([P, HEADS, STORE, DH], F32, name="normed%d" % w) for w in range(2)
                 ]
             rstd = stats.tile([P, 2 * HEADS], F32, name="rstd")
-            nc.vector.reciprocal(rstd[:], std_of[j][:])
-            acc = acc_of[j]
+            nc.vector.reciprocal(rstd[:], std[:])
             for w in range(2):
                 nc.vector.tensor_tensor(
                     out=out_of[group][w][:, :, place, :],
@@ -172,34 +168,17 @@ def tile_pieceroutedattention_pa_t_kernel(
                     op=ALU.mult,
                 )
             if place == STORE - 1:
-                normed = out_of[group]
                 for w in range(2):
                     for s in range(HALVES):
                         first = TILES * s + STORE * group
                         nc.sync.dma_start(
                             out=outs[w][:, :, first : first + STORE, :].rearrange("b h j d -> b h (j d)"),
-                            in_=normed[w][s:P:HALVES, :, :, :].rearrange("p h j d -> p h (j d)"),
+                            in_=out_of[group][w][s:P:HALVES, :, :, :].rearrange("p h j d -> p h (j d)"),
                         )
 
-        for r in range(-1, RUNS + 1):
-            ahead = r + 1 < RUNS
-            here = 0 <= r < RUNS
-            behind = r >= 1
-            if ahead:
-                transpose_run(r + 1)
-            if behind:
-                normalise(RUN * (r - 1))
-            if ahead:
-                copy_out(nc.vector.tensor_copy, r + 1, 0)
-            if here:
-                multiply_run(r)
-            if behind:
-                root_mean_square(RUN * (r - 1) + 1)
-            if ahead:
-                copy_out(nc.scalar.copy, r + 1, 1)
-            if here:
-                root_mean_square(RUN * r)
-            if behind:
-                normalise(RUN * (r - 1) + 1)
-            if ahead:
-                quantise_run(r + 1)
+        for j in range(LOOKAHEAD):
+            prepare(j)
+        for j in range(TILES):
+            if j + LOOKAHEAD < TILES:
+                prepare(j + LOOKAHEAD)
+            project_and_normalise(j)

@@ -169,11 +169,12 @@ def tile_pieceroutedattention_pa_t_kernel(
                 )
             if place == STORE - 1:
                 for w in range(2):
-                    for s in range(HALVES):
-                        first = TILES * s + STORE * group
+                    for h in range(HEADS):
                         nc.sync.dma_start(
-                            out=outs[w][:, :, first : first + STORE, :].rearrange("b h j d -> b h (j d)"),
-                            in_=out_of[group][w][s:P:HALVES, :, :, :].rearrange("p h j d -> p h (j d)"),
+                            out=outs[w][:, h, :, :]
+                            .rearrange("b (s j) d -> b s j d", s=HALVES)[:, :, STORE * group : STORE * (group + 1), :]
+                            .rearrange("b s j d -> b s (j d)"),
+                            in_=out_of[group][w][:, h, :, :].rearrange("p j d -> p (j d)"),
                         )
 
         for j in range(LOOKAHEAD):

@@ -11,6 +11,7 @@ U8 = mybir.dt.uint8
 FP8X4 = mybir.dt.float8_e4m3fn_x4
 ACT = mybir.ActivationFunctionType
 ALU = mybir.AluOpType
+AXIS = mybir.AxisListType
 
 P = 128
 BOARDS = 64
@@ -57,10 +58,9 @@ def tile_pieceroutedattention_pa_t_kernel(
         eps = keep.tile([P, 1], F32)
         nc.vector.memset(eps[:], EPS)
         warm = keep.tile([P, 1], F32)
-        nc.scalar.activation(out=warm[:], in_=eps[:], func=ACT.Sqrt)
+        nc.scalar.activation(out=warm[:], in_=eps[:], func=ACT.Abs_reciprocal_sqrt)
         ident = keep.tile([P, P], F32)
         make_identity(nc, ident[:])
-        squares = keep.tile([P, DH], BF16)
 
         x_tiles = []
 
@@ -91,6 +91,8 @@ def tile_pieceroutedattention_pa_t_kernel(
 
         grouped_of = {}
         codes_of = {}
+        acc_of = {}
+        stat_of = {}
         out_of = {}
 
         def prepare(j):
@@ -124,15 +126,15 @@ def tile_pieceroutedattention_pa_t_kernel(
                 )
                 codes_of[pair] = (codes, plane)
 
-        def project_and_normalise(j):
+        def multiply(j):
             pair, i = divmod(j, PAIR)
             codes, plane = codes_of[pair]
-            acc = []
+            acc_of[j] = []
             for w in range(2):
-                acc.append(banks.tile([P, E], F32, name="acc", tag="bank"))
+                acc = banks.tile([P, E], F32, name="acc", tag="bank")
                 for g in range(PASSES):
                     nc.tensor.matmul_mx(
-                        out=acc[w][:],
+                        out=acc[:],
                         lhsT=codes[:, i, g, :].bitcast(FP8X4),
                         lhsT_scale=plane[:, i, g, :],
                         rhs=w_words[:, w, g, :].bitcast(FP8X4),
@@ -140,33 +142,47 @@ def tile_pieceroutedattention_pa_t_kernel(
                         start=(g == 0),
                         stop=(g == PASSES - 1),
                     )
+                acc_of[j].append(acc)
+            stat_of[j] = stats.tile([P, 2 * HEADS, 2, 3], F32, name="stat")
 
+        def head_statistics(j, w):
+            for h in range(HEADS):
+                nc.vector.bn_stats(
+                    out=stat_of[j][:, HEADS * w + h, :, :].rearrange("p e s -> p (e s)"),
+                    in_=acc_of[j][w][:, DH * h : DH * (h + 1)],
+                )
+
+        def square_means(j):
+            stat = stat_of[j]
+            nc.vector.scalar_tensor_tensor(
+                out=stat[:, :, :, 0],
+                in0=stat[:, :, :, 1],
+                scalar=DH / 2.0,
+                in1=stat[:, :, :, 1],
+                op0=ALU.mult,
+                op1=ALU.mult,
+            )
+
+        def normalise(j):
             sums = stats.tile([P, 2 * HEADS], F32, name="sums")
-            for w in range(2):
-                for h in range(HEADS):
-                    nc.scalar.activation(
-                        out=squares[:],
-                        in_=acc[w][:, DH * h : DH * (h + 1)],
-                        func=ACT.Square,
-                        accum_out=sums[:, HEADS * w + h : HEADS * w + h + 1],
-                    )
-            std = stats.tile([P, 2 * HEADS], F32, name="std")
-            nc.scalar.activation(out=std[:], in_=sums[:], func=ACT.Sqrt, bias=eps[:], scale=1.0 / DH)
-
+            nc.vector.tensor_reduce(out=sums[:], in_=stat_of[j][:, :, :, 0:3:2], axis=AXIS.XY, op=ALU.add)
+            rstd = stats.tile([P, 2 * HEADS], F32, name="rstd")
+            nc.scalar.activation(
+                out=rstd[:], in_=sums[:], func=ACT.Abs_reciprocal_sqrt, bias=eps[:], scale=1.0 / DH
+            )
             group, place = divmod(j, STORE)
             if place == 0:
                 out_of[group] = [
                     result.tile([P, HEADS, STORE, DH], F32, name="normed%d" % w) for w in range(2)
                 ]
-            rstd = stats.tile([P, 2 * HEADS], F32, name="rstd")
-            nc.vector.reciprocal(rstd[:], std[:])
             for w in range(2):
-                nc.vector.tensor_tensor(
-                    out=out_of[group][w][:, :, place, :],
-                    in0=acc[w][:].rearrange("p (h d) -> p h d", h=HEADS),
-                    in1=rstd[:, HEADS * w : HEADS * (w + 1)].unsqueeze(2).to_broadcast([P, HEADS, DH]),
-                    op=ALU.mult,
-                )
+                for h in range(HEADS):
+                    nc.scalar.activation(
+                        out=out_of[group][w][:, h, place, :],
+                        in_=acc_of[j][w][:, DH * h : DH * (h + 1)],
+                        func=ACT.Copy,
+                        scale=rstd[:, HEADS * w + h : HEADS * w + h + 1],
+                    )
             if place == STORE - 1:
                 for w in range(2):
                     for h in range(HEADS):
@@ -179,7 +195,15 @@ def tile_pieceroutedattention_pa_t_kernel(
 
         for j in range(LOOKAHEAD):
             prepare(j)
-        for j in range(TILES):
+        for j in range(TILES + 1):
             if j + LOOKAHEAD < TILES:
                 prepare(j + LOOKAHEAD)
-            project_and_normalise(j)
+            if j < TILES:
+                multiply(j)
+                head_statistics(j, 0)
+            if j > 0:
+                square_means(j - 1)
+            if j < TILES:
+                head_statistics(j, 1)
+            if j > 0:
+                normalise(j - 1)

@@ -28,7 +28,6 @@ HALVES = SQUARES // TILES
 PAIR = 2
 PAIRS = TILES // PAIR
 STORE = 4
-LOOKAHEAD = 32
 VECTOR_COPIES_ONE_IN = 4
 PSUM_BANKS = 8
 
@@ -93,6 +92,8 @@ def tile_pieceroutedattention_pa_t_kernel(
         codes_of = {}
         acc_of = {}
         stat_of = {}
+        sums_of = {}
+        rstd_of = {}
         out_of = {}
 
         def prepare(j):
@@ -145,12 +146,12 @@ def tile_pieceroutedattention_pa_t_kernel(
                 acc_of[j].append(acc)
             stat_of[j] = stats.tile([P, 2 * HEADS, 2, 3], F32, name="stat")
 
-        def head_statistics(j, w):
-            for h in range(HEADS):
-                nc.vector.bn_stats(
-                    out=stat_of[j][:, HEADS * w + h, :, :].rearrange("p e s -> p (e s)"),
-                    in_=acc_of[j][w][:, DH * h : DH * (h + 1)],
-                )
+        def head_statistics(j, c):
+            w, h = divmod(c, HEADS)
+            nc.vector.bn_stats(
+                out=stat_of[j][:, c, :, :].rearrange("p e s -> p (e s)"),
+                in_=acc_of[j][w][:, DH * h : DH * (h + 1)],
+            )
 
         def square_means(j):
             stat = stat_of[j]
@@ -163,47 +164,58 @@ def tile_pieceroutedattention_pa_t_kernel(
                 op1=ALU.mult,
             )
 
-        def normalise(j):
-            sums = stats.tile([P, 2 * HEADS], F32, name="sums")
-            nc.vector.tensor_reduce(out=sums[:], in_=stat_of[j][:, :, :, 0:3:2], axis=AXIS.XY, op=ALU.add)
-            rstd = stats.tile([P, 2 * HEADS], F32, name="rstd")
-            nc.scalar.activation(
-                out=rstd[:], in_=sums[:], func=ACT.Abs_reciprocal_sqrt, bias=eps[:], scale=1.0 / DH
+        def sum_squares(j):
+            sums_of[j] = stats.tile([P, 2 * HEADS], F32, name="sums")
+            nc.vector.tensor_reduce(
+                out=sums_of[j][:], in_=stat_of[j][:, :, :, 0:3:2], axis=AXIS.XY, op=ALU.add
             )
+
+        def reciprocal_root(j):
+            rstd_of[j] = stats.tile([P, 2 * HEADS], F32, name="rstd")
+            nc.scalar.activation(
+                out=rstd_of[j][:],
+                in_=sums_of[j][:],
+                func=ACT.Abs_reciprocal_sqrt,
+                bias=eps[:],
+                scale=1.0 / DH,
+            )
+
+        def normalise(j, w):
             group, place = divmod(j, STORE)
             if place == 0:
-                out_of[group] = [
-                    result.tile([P, HEADS, STORE, DH], F32, name="normed%d" % w) for w in range(2)
-                ]
-            for w in range(2):
-                for h in range(HEADS):
-                    nc.scalar.activation(
-                        out=out_of[group][w][:, h, place, :],
-                        in_=acc_of[j][w][:, DH * h : DH * (h + 1)],
-                        func=ACT.Copy,
-                        scale=rstd[:, HEADS * w + h : HEADS * w + h + 1],
-                    )
+                out_of[(group, w)] = result.tile([P, HEADS, STORE, DH], F32, name="normed%d" % w)
+            normed = out_of[(group, w)]
+            for h in range(HEADS):
+                nc.scalar.activation(
+                    out=normed[:, h, place, :],
+                    in_=acc_of[j][w][:, DH * h : DH * (h + 1)],
+                    func=ACT.Copy,
+                    scale=rstd_of[j][:, HEADS * w + h : HEADS * w + h + 1],
+                )
             if place == STORE - 1:
-                for w in range(2):
-                    for h in range(HEADS):
-                        nc.sync.dma_start(
-                            out=outs[w][:, h, :, :]
-                            .rearrange("b (s j) d -> b s j d", s=HALVES)[:, :, STORE * group : STORE * (group + 1), :]
-                            .rearrange("b s j d -> b s (j d)"),
-                            in_=out_of[group][w][:, h, :, :].rearrange("p j d -> p (j d)"),
-                        )
+                for h in range(HEADS):
+                    nc.sync.dma_start(
+                        out=outs[w][:, h, :, :]
+                        .rearrange("b (s j) d -> b s j d", s=HALVES)[:, :, STORE * group : STORE * (group + 1), :]
+                        .rearrange("b s j d -> b s (j d)"),
+                        in_=normed[:, h, :, :].rearrange("p j d -> p (j d)"),
+                    )
 
-        for j in range(LOOKAHEAD):
+        for j in range(TILES):
             prepare(j)
-        for j in range(TILES + 1):
-            if j + LOOKAHEAD < TILES:
-                prepare(j + LOOKAHEAD)
+        for j in range(TILES + 2):
             if j < TILES:
                 multiply(j)
-                head_statistics(j, 0)
-            if j > 0:
-                square_means(j - 1)
-            if j < TILES:
-                head_statistics(j, 1)
-            if j > 0:
-                normalise(j - 1)
+            for c in range(2 * HEADS):
+                if j < TILES:
+                    head_statistics(j, c)
+                if c == 1 and 1 <= j <= TILES:
+                    square_means(j - 1)
+                if c == 3 and 1 <= j <= TILES:
+                    sum_squares(j - 1)
+            if 1 <= j <= TILES:
+                reciprocal_root(j - 1)
+            if j >= 2:
+                normalise(j - 2, 1)
+            if 1 <= j <= TILES:
+                normalise(j - 1, 0)

@@ -29,6 +29,7 @@ PAIR = 2
 PAIRS = TILES // PAIR
 STORE = 4
 VECTOR_COPIES_ONE_IN = 4
+VECTOR_NORMALISES_ONE_IN = 4
 PSUM_BANKS = 8
 
 FLOPS = 2 * BOARDS * SQUARES * C * 2 * E
@@ -180,26 +181,43 @@ def tile_pieceroutedattention_pa_t_kernel(
                 scale=1.0 / DH,
             )
 
-        def normalise(j, w):
+        def result_row(j, w):
             group, place = divmod(j, STORE)
             if place == 0:
                 out_of[(group, w)] = result.tile([P, HEADS, STORE, DH], F32, name="normed%d" % w)
-            normed = out_of[(group, w)]
+            return out_of[(group, w)][:, :, place, :]
+
+        def normalise_on_scalar(j, w):
+            row = result_row(j, w)
             for h in range(HEADS):
                 nc.scalar.activation(
-                    out=normed[:, h, place, :],
+                    out=row[:, h, :],
                     in_=acc_of[j][w][:, DH * h : DH * (h + 1)],
                     func=ACT.Copy,
                     scale=rstd_of[j][:, HEADS * w + h : HEADS * w + h + 1],
                 )
+
+        def normalise_on_vector(j, w):
+            nc.vector.tensor_tensor(
+                out=result_row(j, w),
+                in0=acc_of[j][w][:].rearrange("p (h d) -> p h d", h=HEADS),
+                in1=rstd_of[j][:, HEADS * w : HEADS * (w + 1)].unsqueeze(2).to_broadcast([P, HEADS, DH]),
+                op=ALU.mult,
+            )
+
+        def store_if_complete(j, w):
+            group, place = divmod(j, STORE)
             if place == STORE - 1:
                 for h in range(HEADS):
                     nc.sync.dma_start(
                         out=outs[w][:, h, :, :]
                         .rearrange("b (s j) d -> b s j d", s=HALVES)[:, :, STORE * group : STORE * (group + 1), :]
                         .rearrange("b s j d -> b s (j d)"),
-                        in_=normed[:, h, :, :].rearrange("p j d -> p (j d)"),
+                        in_=out_of[(group, w)][:, h, :, :].rearrange("p j d -> p (j d)"),
                     )
+
+        def key_bank_is_vectors(j):
+            return j % VECTOR_NORMALISES_ONE_IN == VECTOR_NORMALISES_ONE_IN - 1
 
         for j in range(TILES):
             prepare(j)
@@ -213,9 +231,14 @@ def tile_pieceroutedattention_pa_t_kernel(
                     square_means(j - 1)
                 if c == 3 and 1 <= j <= TILES:
                     sum_squares(j - 1)
+                if c == 5 and j >= 2 and key_bank_is_vectors(j - 2):
+                    normalise_on_vector(j - 2, 1)
             if 1 <= j <= TILES:
                 reciprocal_root(j - 1)
             if j >= 2:
-                normalise(j - 2, 1)
+                if not key_bank_is_vectors(j - 2):
+                    normalise_on_scalar(j - 2, 1)
+                store_if_complete(j - 2, 1)
             if 1 <= j <= TILES:
-                normalise(j - 1, 0)
+                normalise_on_scalar(j - 1, 0)
+                store_if_complete(j - 1, 0)

@@ -28,8 +28,7 @@ HALVES = SQUARES // TILES
 PAIR = 2
 PAIRS = TILES // PAIR
 STORE = 4
-VECTOR_COPIES_ONE_IN = 4
-VECTOR_NORMALISES_ONE_IN = 4
+AHEAD = 2
 PSUM_BANKS = 8
 
 FLOPS = 2 * BOARDS * SQUARES * C * 2 * E
@@ -89,6 +88,7 @@ def tile_pieceroutedattention_pa_t_kernel(
         for pair in range(1, PAIRS):
             load_x(pair)
 
+        xt_of = {}
         grouped_of = {}
         codes_of = {}
         acc_of = {}
@@ -97,36 +97,37 @@ def tile_pieceroutedattention_pa_t_kernel(
         rstd_of = {}
         out_of = {}
 
-        def prepare(j):
-            pair, i = divmod(j, PAIR)
+        def transpose_pair(pair):
             words = x_tiles[pair][:].bitcast(F32)
-            xt = banks.tile([P, 2 * PASSES, P], F32, name="xt", tag="bank")
-            for g in range(PASSES):
-                for u in range(2):
-                    nc.tensor.transpose(
-                        xt[:, 2 * g + u, :], words[:, i, 256 * g + u : 256 * (g + 1) : 2], ident[:]
-                    )
-            if i == 0:
-                grouped_of[pair] = stage.tile(
-                    [P, PAIR, PASSES, P, 4], BF16, name="grouped", align_bytes=64
-                )
-            copy_out = nc.vector.tensor_copy if j % VECTOR_COPIES_ONE_IN == 0 else nc.scalar.copy
-            copy_out(
+            for i in range(PAIR):
+                xt = banks.tile([P, 2 * PASSES, P], F32, name="xt", tag="bank")
+                for g in range(PASSES):
+                    for u in range(2):
+                        nc.tensor.transpose(
+                            xt[:, 2 * g + u, :], words[:, i, 256 * g + u : 256 * (g + 1) : 2], ident[:]
+                        )
+                xt_of[PAIR * pair + i] = xt
+            grouped_of[pair] = stage.tile([P, PAIR, PASSES, P, 4], BF16, name="grouped", align_bytes=64)
+
+        def copy_out(pair, i):
+            engine_copy = nc.vector.tensor_copy if (i == 0 and pair % 2 == 0) else nc.scalar.copy
+            engine_copy(
                 out=grouped_of[pair][:, i, :, :, :]
                 .rearrange("p g n t -> p (g n t)")
                 .bitcast(F32)
                 .rearrange("p (g n u) -> p g n u", g=PASSES, u=2),
-                in_=xt[:].rearrange("p (g u) n -> p g n u", u=2),
+                in_=xt_of[PAIR * pair + i][:].rearrange("p (g u) n -> p g n u", u=2),
             )
-            if i == PAIR - 1:
-                codes = mx_pool.tile([P, PAIR, PASSES, P], U32, name="codes", align_bytes=64)
-                plane = mx_pool.tile([P, PAIR, PASSES, P], U8, name="plane", align_bytes=64)
-                nc.vector.quantize_mx(
-                    out=codes[:].rearrange("p i g n -> p (i g n)").bitcast(FP8X4),
-                    scales=plane[:].rearrange("p i g n -> p (i g n)"),
-                    in_=grouped_of[pair][:].rearrange("p i g n t -> p (i g n t)"),
-                )
-                codes_of[pair] = (codes, plane)
+
+        def quantise_pair(pair):
+            codes = mx_pool.tile([P, PAIR, PASSES, P], U32, name="codes", align_bytes=64)
+            plane = mx_pool.tile([P, PAIR, PASSES, P], U8, name="plane", align_bytes=64)
+            nc.vector.quantize_mx(
+                out=codes[:].rearrange("p i g n -> p (i g n)").bitcast(FP8X4),
+                scales=plane[:].rearrange("p i g n -> p (i g n)"),
+                in_=grouped_of[pair][:].rearrange("p i g n t -> p (i g n t)"),
+            )
+            codes_of[pair] = (codes, plane)
 
         def multiply(j):
             pair, i = divmod(j, PAIR)
@@ -181,47 +182,39 @@ def tile_pieceroutedattention_pa_t_kernel(
                 scale=1.0 / DH,
             )
 
-        def result_row(j, w):
+        def normalise(j, w):
             group, place = divmod(j, STORE)
             if place == 0:
                 out_of[(group, w)] = result.tile([P, HEADS, STORE, DH], F32, name="normed%d" % w)
-            return out_of[(group, w)][:, :, place, :]
-
-        def normalise_on_scalar(j, w):
-            row = result_row(j, w)
+            normed = out_of[(group, w)]
             for h in range(HEADS):
                 nc.scalar.activation(
-                    out=row[:, h, :],
+                    out=normed[:, h, place, :],
                     in_=acc_of[j][w][:, DH * h : DH * (h + 1)],
                     func=ACT.Copy,
                     scale=rstd_of[j][:, HEADS * w + h : HEADS * w + h + 1],
                 )
-
-        def normalise_on_vector(j, w):
-            nc.vector.tensor_tensor(
-                out=result_row(j, w),
-                in0=acc_of[j][w][:].rearrange("p (h d) -> p h d", h=HEADS),
-                in1=rstd_of[j][:, HEADS * w : HEADS * (w + 1)].unsqueeze(2).to_broadcast([P, HEADS, DH]),
-                op=ALU.mult,
-            )
-
-        def store_if_complete(j, w):
-            group, place = divmod(j, STORE)
             if place == STORE - 1:
                 for h in range(HEADS):
                     nc.sync.dma_start(
                         out=outs[w][:, h, :, :]
                         .rearrange("b (s j) d -> b s j d", s=HALVES)[:, :, STORE * group : STORE * (group + 1), :]
                         .rearrange("b s j d -> b s (j d)"),
-                        in_=out_of[(group, w)][:, h, :, :].rearrange("p j d -> p (j d)"),
+                        in_=normed[:, h, :, :].rearrange("p j d -> p (j d)"),
                     )
 
-        def key_bank_is_vectors(j):
-            return j % VECTOR_NORMALISES_ONE_IN == VECTOR_NORMALISES_ONE_IN - 1
-
-        for j in range(TILES):
-            prepare(j)
+        for pair in range(AHEAD):
+            transpose_pair(pair)
+            copy_out(pair, 0)
+            copy_out(pair, 1)
+            quantise_pair(pair)
         for j in range(TILES + 2):
+            pair, i = divmod(j, PAIR)
+            coming = pair + AHEAD
+            if coming < PAIRS and i == 0:
+                transpose_pair(coming)
+                copy_out(coming, 0)
+                copy_out(coming, 1)
             if j < TILES:
                 multiply(j)
             for c in range(2 * HEADS):
@@ -231,14 +224,11 @@ def tile_pieceroutedattention_pa_t_kernel(
                     square_means(j - 1)
                 if c == 3 and 1 <= j <= TILES:
                     sum_squares(j - 1)
-                if c == 5 and j >= 2 and key_bank_is_vectors(j - 2):
-                    normalise_on_vector(j - 2, 1)
+            if coming < PAIRS and i == 1:
+                quantise_pair(coming)
             if 1 <= j <= TILES:
                 reciprocal_root(j - 1)
             if j >= 2:
-                if not key_bank_is_vectors(j - 2):
-                    normalise_on_scalar(j - 2, 1)
-                store_if_complete(j - 2, 1)
+                normalise(j - 2, 1)
             if 1 <= j <= TILES:
-                normalise_on_scalar(j - 1, 0)
-                store_if_complete(j - 1, 0)
+                normalise(j - 1, 0)

@@ -62,6 +62,7 @@ def tile_pieceroutedattention_pa_t_kernel(
         make_identity(nc, ident[:])
 
         x_tiles = []
+        w_words = keep.tile([P, 2, PASSES, E], U32, align_bytes=64)
 
         def load_x(pair):
             x_pair = x_pool.tile([P, PAIR, C], BF16, name="x_pair")
@@ -70,22 +71,29 @@ def tile_pieceroutedattention_pa_t_kernel(
             )
             x_tiles.append(x_pair)
 
-        load_x(0)
-        w_words = keep.tile([P, 2, PASSES, E], U32, align_bytes=64)
-        for w in range(2):
+        def load_words(w):
             nc.sync.dma_start(
                 out=w_words[:, w, :, :].bitcast(I32),
                 in_=weights[w][0].rearrange("g p n t -> p g (n t)").bitcast(I32),
             )
-        for w in range(2):
-            for quadrant in range(4):
-                nc.sync.dma_start(
-                    out=w_planes[32 * quadrant : 32 * quadrant + 4, w, :, :].bitcast(I32),
-                    in_=weights[w][1][:, 4 * quadrant : 4 * quadrant + 4, :]
-                    .rearrange("g r n -> r g n")
-                    .bitcast(I32),
-                )
-        for pair in range(1, PAIRS):
+
+        def load_scale_rows(w, quadrant):
+            nc.sync.dma_start(
+                out=w_planes[32 * quadrant : 32 * quadrant + 4, w, :, :].bitcast(I32),
+                in_=weights[w][1][:, 4 * quadrant : 4 * quadrant + 4, :]
+                .rearrange("g r n -> r g n")
+                .bitcast(I32),
+            )
+
+        for pair in range(AHEAD + 1):
+            load_x(pair)
+            load_scale_rows(pair // 2, 2 * (pair % 2))
+            load_scale_rows(pair // 2, 2 * (pair % 2) + 1)
+        load_words(0)
+        load_scale_rows(1, 2)
+        load_scale_rows(1, 3)
+        load_words(1)
+        for pair in range(AHEAD + 1, PAIRS):
             load_x(pair)
 
         xt_of = {}

@@ -154,13 +154,13 @@ def tile_pieceroutedattention_pa_t_kernel(
                         stop=(g == PASSES - 1),
                     )
                 acc_of[j].append(acc)
-            stat_of[j] = stats.tile([P, 2 * HEADS, 2, 3], F32, name="stat")
+            stat_of[j] = stats.tile([P, HEADS, 2, 3], F32, name="stat")
 
         def head_statistics(j, c):
-            w, h = divmod(c, HEADS)
+            w, a = divmod(c, HEADS // 2)
             nc.vector.bn_stats(
                 out=stat_of[j][:, c, :, :].rearrange("p e s -> p (e s)"),
-                in_=acc_of[j][w][:, DH * h : DH * (h + 1)],
+                in_=acc_of[j][w][:, 2 * DH * a : 2 * DH * (a + 1)].rearrange("p (e d) -> p d e", e=2),
             )
 
         def square_means(j):
@@ -168,7 +168,7 @@ def tile_pieceroutedattention_pa_t_kernel(
             nc.vector.scalar_tensor_tensor(
                 out=stat[:, :, :, 0],
                 in0=stat[:, :, :, 1],
-                scalar=DH / 2.0,
+                scalar=float(DH),
                 in1=stat[:, :, :, 1],
                 op0=ALU.mult,
                 op1=ALU.mult,
@@ -177,7 +177,10 @@ def tile_pieceroutedattention_pa_t_kernel(
         def sum_squares(j):
             sums_of[j] = stats.tile([P, 2 * HEADS], F32, name="sums")
             nc.vector.tensor_reduce(
-                out=sums_of[j][:], in_=stat_of[j][:, :, :, 0:3:2], axis=AXIS.XY, op=ALU.add
+                out=sums_of[j][:],
+                in_=stat_of[j][:].rearrange("p c e s -> p (c e) s")[:, :, 0:3:2],
+                axis=AXIS.X,
+                op=ALU.add,
             )
 
         def reciprocal_root(j):
@@ -225,12 +228,12 @@ def tile_pieceroutedattention_pa_t_kernel(
                 copy_out(coming, 1)
             if j < TILES:
                 multiply(j)
-            for c in range(2 * HEADS):
+            for c in range(HEADS):
                 if j < TILES:
                     head_statistics(j, c)
-                if c == 1 and 1 <= j <= TILES:
+                if c == 0 and 1 <= j <= TILES:
                     square_means(j - 1)
-                if c == 3 and 1 <= j <= TILES:
+                if c == 1 and 1 <= j <= TILES:
                     sum_squares(j - 1)
             if coming < PAIRS and i == 1:
                 quantise_pair(coming)

@@ -49,6 +49,7 @@ def tile_pieceroutedattention_pa_t_kernel(
         stage = stack.enter_context(tc.tile_pool(name="stage", bufs=3))
         mx_pool = stack.enter_context(tc.tile_pool(name="mx", bufs=PAIRS))
         stats = stack.enter_context(tc.tile_pool(name="stats", bufs=4))
+        scrap = stack.enter_context(tc.tile_pool(name="scrap", bufs=4))
         result = stack.enter_context(tc.tile_pool(name="result", bufs=3))
         banks = stack.enter_context(tc.psum_pool(name="banks", bufs=PSUM_BANKS))
 
@@ -100,7 +101,6 @@ def tile_pieceroutedattention_pa_t_kernel(
         grouped_of = {}
         codes_of = {}
         acc_of = {}
-        stat_of = {}
         sums_of = {}
         rstd_of = {}
         out_of = {}
@@ -118,7 +118,7 @@ def tile_pieceroutedattention_pa_t_kernel(
             grouped_of[pair] = stage.tile([P, PAIR, PASSES, P, 4], BF16, name="grouped", align_bytes=64)
 
         def copy_out(pair, i):
-            engine_copy = nc.vector.tensor_copy if (i == 0 and pair % 2 == 0) else nc.scalar.copy
+            engine_copy = nc.vector.tensor_copy if i == 0 else nc.scalar.copy
             engine_copy(
                 out=grouped_of[pair][:, i, :, :, :]
                 .rearrange("p g n t -> p (g n t)")
@@ -154,33 +154,16 @@ def tile_pieceroutedattention_pa_t_kernel(
                         stop=(g == PASSES - 1),
                     )
                 acc_of[j].append(acc)
-            stat_of[j] = stats.tile([P, HEADS, 2, 3], F32, name="stat")
-
-        def head_statistics(j, c):
-            w, a = divmod(c, HEADS // 2)
-            nc.vector.bn_stats(
-                out=stat_of[j][:, c, :, :].rearrange("p e s -> p (e s)"),
-                in_=acc_of[j][w][:, 2 * DH * a : 2 * DH * (a + 1)].rearrange("p (e d) -> p d e", e=2),
-            )
-
-        def square_means(j):
-            stat = stat_of[j]
-            nc.vector.scalar_tensor_tensor(
-                out=stat[:, :, :, 0],
-                in0=stat[:, :, :, 1],
-                scalar=float(DH),
-                in1=stat[:, :, :, 1],
-                op0=ALU.mult,
-                op1=ALU.mult,
-            )
-
-        def sum_squares(j):
             sums_of[j] = stats.tile([P, 2 * HEADS], F32, name="sums")
-            nc.vector.tensor_reduce(
-                out=sums_of[j][:],
-                in_=stat_of[j][:].rearrange("p c e s -> p (c e) s")[:, :, 0:3:2],
-                axis=AXIS.X,
-                op=ALU.add,
+
+        def head_square_sum(j, c):
+            w, h = divmod(c, HEADS)
+            squares = scrap.tile([P, DH], BF16, name="squares")
+            nc.scalar.activation(
+                out=squares[:],
+                in_=acc_of[j][w][:, DH * h : DH * (h + 1)],
+                func=ACT.Square,
+                accum_out=sums_of[j][:, c : c + 1],
             )
 
         def reciprocal_root(j):
@@ -198,13 +181,12 @@ def tile_pieceroutedattention_pa_t_kernel(
             if place == 0:
                 out_of[(group, w)] = result.tile([P, HEADS, STORE, DH], F32, name="normed%d" % w)
             normed = out_of[(group, w)]
-            for h in range(HEADS):
-                nc.scalar.activation(
-                    out=normed[:, h, place, :],
-                    in_=acc_of[j][w][:, DH * h : DH * (h + 1)],
-                    func=ACT.Copy,
-                    scale=rstd_of[j][:, HEADS * w + h : HEADS * w + h + 1],
-                )
+            nc.vector.tensor_tensor(
+                out=normed[:, :, place, :],
+                in0=acc_of[j][w][:].rearrange("p (h d) -> p h d", h=HEADS),
+                in1=rstd_of[j][:, HEADS * w : HEADS * (w + 1)].unsqueeze(2).to_broadcast([P, HEADS, DH]),
+                op=ALU.mult,
+            )
             if place == STORE - 1:
                 for h in range(HEADS):
                     nc.sync.dma_start(
@@ -219,27 +201,29 @@ def tile_pieceroutedattention_pa_t_kernel(
             copy_out(pair, 0)
             copy_out(pair, 1)
             quantise_pair(pair)
-        for j in range(TILES + 2):
-            pair, i = divmod(j, PAIR)
+        for pair in range(PAIRS + 1):
+            first, second = PAIR * pair, PAIR * pair + 1
             coming = pair + AHEAD
-            if coming < PAIRS and i == 0:
+            if coming < PAIRS:
                 transpose_pair(coming)
                 copy_out(coming, 0)
                 copy_out(coming, 1)
-            if j < TILES:
-                multiply(j)
-            for c in range(HEADS):
-                if j < TILES:
-                    head_statistics(j, c)
-                if c == 0 and 1 <= j <= TILES:
-                    square_means(j - 1)
-                if c == 1 and 1 <= j <= TILES:
-                    sum_squares(j - 1)
-            if coming < PAIRS and i == 1:
+            if pair >= 1:
+                reciprocal_root(first - 1)
+            if pair < PAIRS:
+                multiply(first)
+                multiply(second)
+                for c in range(2 * HEADS):
+                    head_square_sum(first, c)
+                head_square_sum(second, 0)
+                reciprocal_root(first)
+                for c in range(1, 2 * HEADS):
+                    head_square_sum(second, c)
+            if pair >= 1:
+                normalise(first - 1, 0)
+                normalise(first - 1, 1)
+            if coming < PAIRS:
                 quantise_pair(coming)
-            if 1 <= j <= TILES:
-                reciprocal_root(j - 1)
-            if j >= 2:
-                normalise(j - 2, 1)
-            if 1 <= j <= TILES:
-                normalise(j - 1, 0)
+            if pair < PAIRS:
+                normalise(first, 0)
+                normalise(first, 1)

@@ -28,7 +28,7 @@ HALVES = SQUARES // TILES
 PAIR = 2
 PAIRS = TILES // PAIR
 STORE = 4
-AHEAD = 2
+AHEAD = 1
 PSUM_BANKS = 8
 
 FLOPS = 2 * BOARDS * SQUARES * C * 2 * E
@@ -88,12 +88,12 @@ def tile_pieceroutedattention_pa_t_kernel(
 
         for pair in range(AHEAD + 1):
             load_x(pair)
-            load_scale_rows(pair // 2, 2 * (pair % 2))
-            load_scale_rows(pair // 2, 2 * (pair % 2) + 1)
-        load_words(0)
-        load_scale_rows(1, 2)
-        load_scale_rows(1, 3)
-        load_words(1)
+            load_scale_rows(0, 2 * pair)
+            load_scale_rows(0, 2 * pair + 1)
+        for w in range(2):
+            load_words(w)
+            load_scale_rows(1, 2 * w)
+            load_scale_rows(1, 2 * w + 1)
         for pair in range(AHEAD + 1, PAIRS):
             load_x(pair)
 
@@ -221,9 +221,10 @@ def tile_pieceroutedattention_pa_t_kernel(
                     head_square_sum(second, c)
             if pair >= 1:
                 normalise(first - 1, 0)
-                normalise(first - 1, 1)
             if coming < PAIRS:
                 quantise_pair(coming)
+            if pair >= 1:
+                normalise(first - 1, 1)
             if pair < PAIRS:
                 normalise(first, 0)
                 normalise(first, 1)

@@ -118,7 +118,7 @@ def tile_pieceroutedattention_pa_t_kernel(
             grouped_of[pair] = stage.tile([P, PAIR, PASSES, P, 4], BF16, name="grouped", align_bytes=64)
 
         def copy_out(pair, i):
-            engine_copy = nc.vector.tensor_copy if i == 0 else nc.scalar.copy
+            engine_copy = nc.vector.tensor_copy if (i == 0 or pair % 4 == 1) else nc.scalar.copy
             engine_copy(
                 out=grouped_of[pair][:, i, :, :, :]
                 .rearrange("p g n t -> p (g n t)")

@@ -30,6 +30,7 @@ PAIRS = TILES // PAIR
 STORE = 4
 AHEAD = 1
 PSUM_BANKS = 8
+WORD_BANKS = 2
 
 FLOPS = 2 * BOARDS * SQUARES * C * 2 * E
 
@@ -51,7 +52,8 @@ def tile_pieceroutedattention_pa_t_kernel(
         stats = stack.enter_context(tc.tile_pool(name="stats", bufs=4))
         scrap = stack.enter_context(tc.tile_pool(name="scrap", bufs=4))
         result = stack.enter_context(tc.tile_pool(name="result", bufs=3))
-        banks = stack.enter_context(tc.psum_pool(name="banks", bufs=PSUM_BANKS))
+        word_banks = stack.enter_context(tc.psum_pool(name="word_banks", bufs=WORD_BANKS))
+        sum_banks = stack.enter_context(tc.psum_pool(name="sum_banks", bufs=PSUM_BANKS - WORD_BANKS))
 
         w_planes = keep.tile([P, 2, PASSES, E], U8, align_bytes=64)
         nc.vector.memset(w_planes[:].rearrange("p w g n -> p (w g n)").bitcast(I32), 0)
@@ -65,11 +67,14 @@ def tile_pieceroutedattention_pa_t_kernel(
         x_tiles = []
         w_words = keep.tile([P, 2, PASSES, E], U32, align_bytes=64)
 
-        def load_x(pair):
+        def load_x(pair, pieces=1):
             x_pair = x_pool.tile([P, PAIR, C], BF16, name="x_pair")
-            nc.sync.dma_start(
-                out=x_pair[:], in_=x_by_partition[:, PAIR * pair : PAIR * (pair + 1), :]
-            )
+            step = PAIR // pieces
+            for i in range(0, PAIR, step):
+                nc.sync.dma_start(
+                    out=x_pair[:, i : i + step, :],
+                    in_=x_by_partition[:, PAIR * pair + i : PAIR * pair + i + step, :],
+                )
             x_tiles.append(x_pair)
 
         def load_words(w):
@@ -86,15 +91,12 @@ def tile_pieceroutedattention_pa_t_kernel(
                 .bitcast(I32),
             )
 
-        for pair in range(AHEAD + 1):
-            load_x(pair)
-            load_scale_rows(0, 2 * pair)
-            load_scale_rows(0, 2 * pair + 1)
-        for w in range(2):
-            load_words(w)
-            load_scale_rows(1, 2 * w)
-            load_scale_rows(1, 2 * w + 1)
-        for pair in range(AHEAD + 1, PAIRS):
+        for pair in range(2):
+            load_x(pair, pieces=PAIR if pair == 0 else 1)
+            for quadrant in range(4):
+                load_scale_rows(pair, quadrant)
+            load_words(pair)
+        for pair in range(2, PAIRS):
             load_x(pair)
 
         xt_of = {}
@@ -108,7 +110,7 @@ def tile_pieceroutedattention_pa_t_kernel(
         def transpose_pair(pair):
             words = x_tiles[pair][:].bitcast(F32)
             for i in range(PAIR):
-                xt = banks.tile([P, 2 * PASSES, P], F32, name="xt", tag="bank")
+                xt = word_banks.tile([P, 2 * PASSES, P], F32, name="xt", tag="words")
                 for g in range(PASSES):
                     for u in range(2):
                         nc.tensor.transpose(
@@ -127,6 +129,32 @@ def tile_pieceroutedattention_pa_t_kernel(
                 in_=xt_of[PAIR * pair + i][:].rearrange("p (g u) n -> p g n u", u=2),
             )
 
+        def start_tile(i):
+            if i == 0:
+                grouped_of[0] = stage.tile([P, PAIR, PASSES, P, 4], BF16, name="grouped", align_bytes=64)
+                codes = mx_pool.tile([P, PAIR, PASSES, P], U32, name="codes", align_bytes=64)
+                plane = mx_pool.tile([P, PAIR, PASSES, P], U8, name="plane", align_bytes=64)
+                codes_of[0] = (codes, plane)
+            codes, plane = codes_of[0]
+            words = x_tiles[0][:].bitcast(F32)
+            for g in range(PASSES):
+                xt = word_banks.tile([P, 2, P], F32, name="xt", tag="words")
+                for u in range(2):
+                    nc.tensor.transpose(xt[:, u, :], words[:, i, 256 * g + u : 256 * (g + 1) : 2], ident[:])
+                engine_copy = nc.vector.tensor_copy if g == 0 else nc.scalar.copy
+                engine_copy(
+                    out=grouped_of[0][:, i, g, :, :]
+                    .rearrange("p n t -> p (n t)")
+                    .bitcast(F32)
+                    .rearrange("p (n u) -> p n u", u=2),
+                    in_=xt[:].rearrange("p u n -> p n u"),
+                )
+            nc.vector.quantize_mx(
+                out=codes[:, i, :, :].rearrange("p g n -> p (g n)").bitcast(FP8X4),
+                scales=plane[:, i, :, :].rearrange("p g n -> p (g n)"),
+                in_=grouped_of[0][:, i, :, :, :].rearrange("p g n t -> p (g n t)"),
+            )
+
         def quantise_pair(pair):
             codes = mx_pool.tile([P, PAIR, PASSES, P], U32, name="codes", align_bytes=64)
             plane = mx_pool.tile([P, PAIR, PASSES, P], U8, name="plane", align_bytes=64)
@@ -137,12 +165,12 @@ def tile_pieceroutedattention_pa_t_kernel(
             )
             codes_of[pair] = (codes, plane)
 
-        def multiply(j):
+        def multiply(j, projections=(0, 1)):
             pair, i = divmod(j, PAIR)
             codes, plane = codes_of[pair]
-            acc_of[j] = []
-            for w in range(2):
-                acc = banks.tile([P, E], F32, name="acc", tag="bank")
+            acc_of.setdefault(j, [])
+            for w in projections:
+                acc = sum_banks.tile([P, E], F32, name="acc", tag="sums")
                 for g in range(PASSES):
                     nc.tensor.matmul_mx(
                         out=acc[:],
@@ -154,7 +182,8 @@ def tile_pieceroutedattention_pa_t_kernel(
                         stop=(g == PASSES - 1),
                     )
                 acc_of[j].append(acc)
-            sums_of[j] = stats.tile([P, 2 * HEADS], F32, name="sums")
+            if 0 in projections:
+                sums_of[j] = stats.tile([P, 2 * HEADS], F32, name="sums")
 
         def head_square_sum(j, c):
             w, h = divmod(c, HEADS)
@@ -196,12 +225,29 @@ def tile_pieceroutedattention_pa_t_kernel(
                         in_=normed[:, h, :, :].rearrange("p j d -> p (j d)"),
                     )
 
-        for pair in range(AHEAD):
-            transpose_pair(pair)
-            copy_out(pair, 0)
-            copy_out(pair, 1)
-            quantise_pair(pair)
-        for pair in range(PAIRS + 1):
+        start_tile(0)
+        start_tile(1)
+        multiply(0, projections=(0,))
+        multiply(1, projections=(0,))
+        transpose_pair(1)
+        copy_out(1, 0)
+        copy_out(1, 1)
+        multiply(0, projections=(1,))
+        multiply(1, projections=(1,))
+        for c in range(HEADS):
+            head_square_sum(0, c)
+        for c in range(HEADS):
+            head_square_sum(1, c)
+        for c in range(HEADS, 2 * HEADS):
+            head_square_sum(0, c)
+        head_square_sum(1, HEADS)
+        reciprocal_root(0)
+        for c in range(HEADS + 1, 2 * HEADS):
+            head_square_sum(1, c)
+        quantise_pair(1)
+        normalise(0, 0)
+        normalise(0, 1)
+        for pair in range(1, PAIRS + 1):
             first, second = PAIR * pair, PAIR * pair + 1
             coming = pair + AHEAD
             if coming < PAIRS:

@@ -28,6 +28,7 @@ HALVES = SQUARES // TILES
 PAIR = 2
 PAIRS = TILES // PAIR
 STORE = 4
+STORES = (STORE,) * 7 + (2, 2)
 AHEAD = 1
 PSUM_BANKS = 8
 WORD_BANKS = 2
@@ -46,12 +47,13 @@ def tile_pieceroutedattention_pa_t_kernel(
     with ExitStack() as stack:
         stack.enter_context(tc.manual_schedule())
         keep = stack.enter_context(tc.tile_pool(name="keep", bufs=1))
-        x_pool = stack.enter_context(tc.tile_pool(name="x", bufs=PAIRS))
+        x_pool = stack.enter_context(tc.tile_pool(name="x", bufs=10))
         stage = stack.enter_context(tc.tile_pool(name="stage", bufs=3))
-        mx_pool = stack.enter_context(tc.tile_pool(name="mx", bufs=PAIRS))
+        mx_pool = stack.enter_context(tc.tile_pool(name="mx", bufs=4))
         stats = stack.enter_context(tc.tile_pool(name="stats", bufs=4))
         scrap = stack.enter_context(tc.tile_pool(name="scrap", bufs=4))
         result = stack.enter_context(tc.tile_pool(name="result", bufs=3))
+        result_end = stack.enter_context(tc.tile_pool(name="result_end", bufs=2))
         word_banks = stack.enter_context(tc.psum_pool(name="word_banks", bufs=WORD_BANKS))
         sum_banks = stack.enter_context(tc.psum_pool(name="sum_banks", bufs=PSUM_BANKS - WORD_BANKS))
 
@@ -106,6 +108,11 @@ def tile_pieceroutedattention_pa_t_kernel(
         sums_of = {}
         rstd_of = {}
         out_of = {}
+        group_of = {}
+        for size in STORES:
+            start = len(group_of)
+            for i in range(size):
+                group_of[start + i] = (start, size)
 
         def transpose_pair(pair):
             words = x_tiles[pair][:].bitcast(F32)
@@ -206,23 +213,24 @@ def tile_pieceroutedattention_pa_t_kernel(
             )
 
         def normalise(j, w):
-            group, place = divmod(j, STORE)
+            start, size = group_of[j]
+            place = j - start
             if place == 0:
-                out_of[(group, w)] = result.tile([P, HEADS, STORE, DH], F32, name="normed%d" % w)
-            normed = out_of[(group, w)]
+                pool = result if size == STORE else result_end
+                out_of[(start, w)] = pool.tile([P, HEADS, size, DH], F32, name="normed%d" % w)
+            normed = out_of[(start, w)]
             nc.vector.tensor_tensor(
                 out=normed[:, :, place, :],
                 in0=acc_of[j][w][:].rearrange("p (h d) -> p h d", h=HEADS),
                 in1=rstd_of[j][:, HEADS * w : HEADS * (w + 1)].unsqueeze(2).to_broadcast([P, HEADS, DH]),
                 op=ALU.mult,
             )
-            if place == STORE - 1:
-                for h in range(HEADS):
+            if place == size - 1:
+                for s in range(HALVES):
+                    token = TILES * s + start
                     nc.sync.dma_start(
-                        out=outs[w][:, h, :, :]
-                        .rearrange("b (s j) d -> b s j d", s=HALVES)[:, :, STORE * group : STORE * (group + 1), :]
-                        .rearrange("b s j d -> b s (j d)"),
-                        in_=normed[:, h, :, :].rearrange("p j d -> p (j d)"),
+                        out=outs[w][:, :, token : token + size, :].rearrange("b h j d -> b h (j d)"),
+                        in_=normed[s:P:HALVES, :, :, :].rearrange("p h j d -> p h (j d)"),
                     )
 
         start_tile(0)

@@ -63,6 +63,8 @@ def tile_pieceroutedattention_pa_t_kernel(
         nc.vector.memset(eps[:], EPS)
         warm = keep.tile([P, 1], F32)
         nc.scalar.activation(out=warm[:], in_=eps[:], func=ACT.Abs_reciprocal_sqrt)
+        zeros = keep.tile([P, E], BF16)
+        nc.gpsimd.memset(zeros[:].bitcast(F32), 0.0)
         ident = keep.tile([P, P], F32)
         make_identity(nc, ident[:])
 
@@ -135,6 +137,11 @@ def tile_pieceroutedattention_pa_t_kernel(
                 .rearrange("p (g n u) -> p g n u", g=PASSES, u=2),
                 in_=xt_of[PAIR * pair + i][:].rearrange("p (g u) n -> p g n u", u=2),
             )
+
+        def keep_warm(count):
+            idle = sum_banks.tile([P, E], F32, name="idle", tag="sums")
+            for c in range(count):
+                nc.tensor.matmul(idle[:], zeros[:, 0:P], zeros[:], start=True, stop=True)
 
         def start_tile(i):
             if i == 0:
@@ -219,12 +226,21 @@ def tile_pieceroutedattention_pa_t_kernel(
                 pool = result if size == STORE else result_end
                 out_of[(start, w)] = pool.tile([P, HEADS, size, DH], F32, name="normed%d" % w)
             normed = out_of[(start, w)]
-            nc.vector.tensor_tensor(
-                out=normed[:, :, place, :],
-                in0=acc_of[j][w][:].rearrange("p (h d) -> p h d", h=HEADS),
-                in1=rstd_of[j][:, HEADS * w : HEADS * (w + 1)].unsqueeze(2).to_broadcast([P, HEADS, DH]),
-                op=ALU.mult,
-            )
+            if (j, w) == (TILES - 1, 1):
+                for h in range(HEADS):
+                    nc.scalar.activation(
+                        out=normed[:, h, place, :],
+                        in_=acc_of[j][w][:, DH * h : DH * (h + 1)],
+                        func=ACT.Copy,
+                        scale=rstd_of[j][:, HEADS * w + h : HEADS * w + h + 1],
+                    )
+            else:
+                nc.vector.tensor_tensor(
+                    out=normed[:, :, place, :],
+                    in0=acc_of[j][w][:].rearrange("p (h d) -> p h d", h=HEADS),
+                    in1=rstd_of[j][:, HEADS * w : HEADS * (w + 1)].unsqueeze(2).to_broadcast([P, HEADS, DH]),
+                    op=ALU.mult,
+                )
             if place == size - 1:
                 for s in range(HALVES):
                     token = TILES * s + start
@@ -233,8 +249,11 @@ def tile_pieceroutedattention_pa_t_kernel(
                         in_=normed[s:P:HALVES, :, :, :].rearrange("p h j d -> p h (j d)"),
                     )
 
+        keep_warm(4)
         start_tile(0)
+        keep_warm(1)
         start_tile(1)
+        keep_warm(1)
         multiply(0, projections=(0,))
         multiply(1, projections=(0,))
         transpose_pair(1)

@@ -57,16 +57,17 @@ def tile_pieceroutedattention_pa_t_kernel(
         word_banks = stack.enter_context(tc.psum_pool(name="word_banks", bufs=WORD_BANKS))
         sum_banks = stack.enter_context(tc.psum_pool(name="sum_banks", bufs=PSUM_BANKS - WORD_BANKS))
 
+        ident = keep.tile([P, P], F32)
+        nc.vector.memset(ident[:], 0.0)
+        zeros = keep.tile([P, E], BF16)
+        nc.vector.memset(zeros[:].bitcast(F32), 0.0)
         w_planes = keep.tile([P, 2, PASSES, E], U8, align_bytes=64)
         nc.vector.memset(w_planes[:].rearrange("p w g n -> p (w g n)").bitcast(I32), 0)
         eps = keep.tile([P, 1], F32)
         nc.vector.memset(eps[:], EPS)
         warm = keep.tile([P, 1], F32)
         nc.scalar.activation(out=warm[:], in_=eps[:], func=ACT.Abs_reciprocal_sqrt)
-        zeros = keep.tile([P, E], BF16)
-        nc.gpsimd.memset(zeros[:].bitcast(F32), 0.0)
-        ident = keep.tile([P, P], F32)
-        make_identity(nc, ident[:])
+        make_identity(nc, ident[:], nomemset=True)
 
         x_tiles = []
         w_words = keep.tile([P, 2, PASSES, E], U32, align_bytes=64)
@@ -143,25 +144,30 @@ def tile_pieceroutedattention_pa_t_kernel(
             for c in range(count):
                 nc.tensor.matmul(idle[:], zeros[:, 0:P], zeros[:], start=True, stop=True)
 
-        def start_tile(i):
+        def start_transpose(i):
             if i == 0:
                 grouped_of[0] = stage.tile([P, PAIR, PASSES, P, 4], BF16, name="grouped", align_bytes=64)
                 codes = mx_pool.tile([P, PAIR, PASSES, P], U32, name="codes", align_bytes=64)
                 plane = mx_pool.tile([P, PAIR, PASSES, P], U8, name="plane", align_bytes=64)
                 codes_of[0] = (codes, plane)
-            codes, plane = codes_of[0]
             words = x_tiles[0][:].bitcast(F32)
+            xt_of[i] = []
             for g in range(PASSES):
-                xt = word_banks.tile([P, 2, P], F32, name="xt", tag="words")
+                xt = sum_banks.tile([P, 2, P], F32, name="start_xt", tag="sums")
                 for u in range(2):
                     nc.tensor.transpose(xt[:, u, :], words[:, i, 256 * g + u : 256 * (g + 1) : 2], ident[:])
-                engine_copy = nc.vector.tensor_copy if g == 0 else nc.scalar.copy
+                xt_of[i].append(xt)
+
+        def start_quantise(i):
+            codes, plane = codes_of[0]
+            for g in range(PASSES):
+                engine_copy = nc.vector.tensor_copy if (i, g) == (0, 0) else nc.scalar.copy
                 engine_copy(
                     out=grouped_of[0][:, i, g, :, :]
                     .rearrange("p n t -> p (n t)")
                     .bitcast(F32)
                     .rearrange("p (n u) -> p n u", u=2),
-                    in_=xt[:].rearrange("p u n -> p n u"),
+                    in_=xt_of[i][g][:].rearrange("p u n -> p n u"),
                 )
             nc.vector.quantize_mx(
                 out=codes[:, i, :, :].rearrange("p g n -> p (g n)").bitcast(FP8X4),
@@ -249,11 +255,12 @@ def tile_pieceroutedattention_pa_t_kernel(
                         in_=normed[s:P:HALVES, :, :, :].rearrange("p h j d -> p h (j d)"),
                     )
 
-        keep_warm(4)
-        start_tile(0)
-        keep_warm(1)
-        start_tile(1)
-        keep_warm(1)
+        keep_warm(3)
+        start_transpose(0)
+        start_transpose(1)
+        keep_warm(2)
+        start_quantise(0)
+        start_quantise(1)
         multiply(0, projections=(0,))
         multiply(1, projections=(0,))
         transpose_pair(1)

@@ -29,6 +29,7 @@ PAIR = 2
 PAIRS = TILES // PAIR
 STORE = 4
 STORES = (STORE,) * 7 + (2, 2)
+SORT_AHEAD = 2
 AHEAD = 1
 PSUM_BANKS = 8
 WORD_BANKS = 2
@@ -50,6 +51,7 @@ def tile_pieceroutedattention_pa_t_kernel(
         x_pool = stack.enter_context(tc.tile_pool(name="x", bufs=10))
         stage = stack.enter_context(tc.tile_pool(name="stage", bufs=3))
         mx_pool = stack.enter_context(tc.tile_pool(name="mx", bufs=4))
+        sort_pool = stack.enter_context(tc.tile_pool(name="sort", bufs=3))
         stats = stack.enter_context(tc.tile_pool(name="stats", bufs=4))
         scrap = stack.enter_context(tc.tile_pool(name="scrap", bufs=4))
         result = stack.enter_context(tc.tile_pool(name="result", bufs=3))
@@ -105,6 +107,7 @@ def tile_pieceroutedattention_pa_t_kernel(
             load_x(pair)
 
         xt_of = {}
+        sorted_of = {}
         grouped_of = {}
         codes_of = {}
         acc_of = {}
@@ -123,11 +126,27 @@ def tile_pieceroutedattention_pa_t_kernel(
                 xt = word_banks.tile([P, 2 * PASSES, P], F32, name="xt", tag="words")
                 for g in range(PASSES):
                     for u in range(2):
-                        nc.tensor.transpose(
-                            xt[:, 2 * g + u, :], words[:, i, 256 * g + u : 256 * (g + 1) : 2], ident[:]
-                        )
+                        if i == 1 and pair in sorted_of:
+                            picked = sorted_of[pair][:, u, P * g : P * (g + 1), :].rearrange("p w e -> p (w e)").bitcast(F32)
+                        else:
+                            picked = words[:, i, 256 * g + u : 256 * (g + 1) : 2]
+                        nc.tensor.transpose(xt[:, 2 * g + u, :], picked, ident[:])
                 xt_of[PAIR * pair + i] = xt
             grouped_of[pair] = stage.tile([P, PAIR, PASSES, P, 4], BF16, name="grouped", align_bytes=64)
+
+        def sort_second(pair, codes):
+            fence = scrap.tile([P, 1], U32, name="fence")
+            nc.gpsimd.tensor_copy(out=fence[:], in_=codes[:, 0, 0, 0:1])
+            in_order = sort_pool.tile([P, 2, PASSES * P, 2], BF16, name="in_order")
+            nc.gpsimd.tensor_scalar(
+                out=in_order[:],
+                in0=x_tiles[pair][:, 1, :].rearrange("p (w u e) -> p u w e", u=2, e=2),
+                scalar1=1.0,
+                scalar2=0.0,
+                op0=ALU.mult,
+                op1=ALU.add,
+            )
+            sorted_of[pair] = in_order
 
         def copy_out(pair, i):
             engine_copy = nc.vector.tensor_copy if (i == 0 or pair % 4 == 1) else nc.scalar.copy
@@ -184,6 +203,8 @@ def tile_pieceroutedattention_pa_t_kernel(
                 in_=grouped_of[pair][:].rearrange("p i g n t -> p (i g n t)"),
             )
             codes_of[pair] = (codes, plane)
+            if pair + SORT_AHEAD < PAIRS:
+                sort_second(pair + SORT_AHEAD, codes)
 
         def multiply(j, projections=(0, 1)):
             pair, i = divmod(j, PAIR)

from contextlib import ExitStack

import concourse.mybir as mybir
from concourse.masks import make_identity

F32 = mybir.dt.float32
BF16 = mybir.dt.bfloat16
I32 = mybir.dt.int32
U32 = mybir.dt.uint32
U8 = mybir.dt.uint8
FP8X4 = mybir.dt.float8_e4m3fn_x4
ACT = mybir.ActivationFunctionType
ALU = mybir.AluOpType
AXIS = mybir.AxisListType

P = 128
BOARDS = 64
SQUARES = 64
C = 1024
HEADS = 4
DH = 128
E = HEADS * DH
EPS = 2.0 ** -23

PASSES = C // (4 * P)
TILES = BOARDS * SQUARES // P
HALVES = SQUARES // TILES
PAIR = 2
PAIRS = TILES // PAIR
STORE = 4
STORES = (STORE,) * 7 + (2, 2)
SORT_AHEAD = 2
AHEAD = 1
PSUM_BANKS = 8
WORD_BANKS = 2

FLOPS = 2 * BOARDS * SQUARES * C * 2 * E


def tile_pieceroutedattention_pa_t_kernel(
    tc, x, Wq_words, Wq_scales, Wk_words, Wk_scales, out_0, out_1
):
    nc = tc.nc
    weights = ((Wq_words, Wq_scales), (Wk_words, Wk_scales))
    outs = (out_0, out_1)
    x_by_partition = x.rearrange("b (s j) c -> (b s) j c", s=HALVES)

    with ExitStack() as stack:
        stack.enter_context(tc.manual_schedule())
        keep = stack.enter_context(tc.tile_pool(name="keep", bufs=1))
        x_pool = stack.enter_context(tc.tile_pool(name="x", bufs=10))
        stage = stack.enter_context(tc.tile_pool(name="stage", bufs=3))
        mx_pool = stack.enter_context(tc.tile_pool(name="mx", bufs=4))
        sort_pool = stack.enter_context(tc.tile_pool(name="sort", bufs=3))
        stats = stack.enter_context(tc.tile_pool(name="stats", bufs=4))
        scrap = stack.enter_context(tc.tile_pool(name="scrap", bufs=4))
        result = stack.enter_context(tc.tile_pool(name="result", bufs=3))
        result_end = stack.enter_context(tc.tile_pool(name="result_end", bufs=2))
        word_banks = stack.enter_context(tc.psum_pool(name="word_banks", bufs=WORD_BANKS))
        sum_banks = stack.enter_context(tc.psum_pool(name="sum_banks", bufs=PSUM_BANKS - WORD_BANKS))

        ident = keep.tile([P, P], F32)
        nc.vector.memset(ident[:], 0.0)
        zeros = keep.tile([P, E], BF16)
        nc.vector.memset(zeros[:].bitcast(F32), 0.0)
        w_planes = keep.tile([P, 2, PASSES, E], U8, align_bytes=64)
        nc.vector.memset(w_planes[:].rearrange("p w g n -> p (w g n)").bitcast(I32), 0)
        eps = keep.tile([P, 1], F32)
        nc.vector.memset(eps[:], EPS)
        warm = keep.tile([P, 1], F32)
        nc.scalar.activation(out=warm[:], in_=eps[:], func=ACT.Abs_reciprocal_sqrt)
        make_identity(nc, ident[:], nomemset=True)

        x_tiles = []
        w_words = keep.tile([P, 2, PASSES, E], U32, align_bytes=64)

        def load_x(pair, pieces=1):
            x_pair = x_pool.tile([P, PAIR, C], BF16, name="x_pair")
            step = PAIR // pieces
            for i in range(0, PAIR, step):
                nc.sync.dma_start(
                    out=x_pair[:, i : i + step, :],
                    in_=x_by_partition[:, PAIR * pair + i : PAIR * pair + i + step, :],
                )
            x_tiles.append(x_pair)

        def load_words(w):
            nc.sync.dma_start(
                out=w_words[:, w, :, :].bitcast(I32),
                in_=weights[w][0].rearrange("g p n t -> p g (n t)").bitcast(I32),
            )

        def load_scale_rows(w, quadrant):
            nc.sync.dma_start(
                out=w_planes[32 * quadrant : 32 * quadrant + 4, w, :, :].bitcast(I32),
                in_=weights[w][1][:, 4 * quadrant : 4 * quadrant + 4, :]
                .rearrange("g r n -> r g n")
                .bitcast(I32),
            )

        for pair in range(2):
            load_x(pair, pieces=PAIR if pair == 0 else 1)
            for quadrant in range(4):
                load_scale_rows(pair, quadrant)
            load_words(pair)
        for pair in range(2, PAIRS):
            load_x(pair)

        xt_of = {}
        sorted_of = {}
        grouped_of = {}
        codes_of = {}
        acc_of = {}
        sums_of = {}
        rstd_of = {}
        out_of = {}
        group_of = {}
        for size in STORES:
            start = len(group_of)
            for i in range(size):
                group_of[start + i] = (start, size)

        def transpose_pair(pair):
            words = x_tiles[pair][:].bitcast(F32)
            for i in range(PAIR):
                xt = word_banks.tile([P, 2 * PASSES, P], F32, name="xt", tag="words")
                for g in range(PASSES):
                    for u in range(2):
                        if i == 1 and pair in sorted_of:
                            picked = sorted_of[pair][:, u, P * g : P * (g + 1), :].rearrange("p w e -> p (w e)").bitcast(F32)
                        else:
                            picked = words[:, i, 256 * g + u : 256 * (g + 1) : 2]
                        nc.tensor.transpose(xt[:, 2 * g + u, :], picked, ident[:])
                xt_of[PAIR * pair + i] = xt
            grouped_of[pair] = stage.tile([P, PAIR, PASSES, P, 4], BF16, name="grouped", align_bytes=64)

        def sort_second(pair, codes):
            fence = scrap.tile([P, 1], U32, name="fence")
            nc.gpsimd.tensor_copy(out=fence[:], in_=codes[:, 0, 0, 0:1])
            in_order = sort_pool.tile([P, 2, PASSES * P, 2], BF16, name="in_order")
            nc.gpsimd.tensor_scalar(
                out=in_order[:],
                in0=x_tiles[pair][:, 1, :].rearrange("p (w u e) -> p u w e", u=2, e=2),
                scalar1=1.0,
                scalar2=0.0,
                op0=ALU.mult,
                op1=ALU.add,
            )
            sorted_of[pair] = in_order

        def copy_out(pair, i):
            engine_copy = nc.vector.tensor_copy if (i == 0 or pair % 4 == 1) else nc.scalar.copy
            engine_copy(
                out=grouped_of[pair][:, i, :, :, :]
                .rearrange("p g n t -> p (g n t)")
                .bitcast(F32)
                .rearrange("p (g n u) -> p g n u", g=PASSES, u=2),
                in_=xt_of[PAIR * pair + i][:].rearrange("p (g u) n -> p g n u", u=2),
            )

        def keep_warm(count):
            idle = sum_banks.tile([P, E], F32, name="idle", tag="sums")
            for c in range(count):
                nc.tensor.matmul(idle[:], zeros[:, 0:P], zeros[:], start=True, stop=True)

        def start_transpose(i):
            if i == 0:
                grouped_of[0] = stage.tile([P, PAIR, PASSES, P, 4], BF16, name="grouped", align_bytes=64)
                codes = mx_pool.tile([P, PAIR, PASSES, P], U32, name="codes", align_bytes=64)
                plane = mx_pool.tile([P, PAIR, PASSES, P], U8, name="plane", align_bytes=64)
                codes_of[0] = (codes, plane)
            words = x_tiles[0][:].bitcast(F32)
            xt_of[i] = []
            for g in range(PASSES):
                xt = sum_banks.tile([P, 2, P], F32, name="start_xt", tag="sums")
                for u in range(2):
                    nc.tensor.transpose(xt[:, u, :], words[:, i, 256 * g + u : 256 * (g + 1) : 2], ident[:])
                xt_of[i].append(xt)

        def start_quantise(i):
            codes, plane = codes_of[0]
            for g in range(PASSES):
                engine_copy = nc.vector.tensor_copy if (i, g) == (0, 0) else nc.scalar.copy
                engine_copy(
                    out=grouped_of[0][:, i, g, :, :]
                    .rearrange("p n t -> p (n t)")
                    .bitcast(F32)
                    .rearrange("p (n u) -> p n u", u=2),
                    in_=xt_of[i][g][:].rearrange("p u n -> p n u"),
                )
            nc.vector.quantize_mx(
                out=codes[:, i, :, :].rearrange("p g n -> p (g n)").bitcast(FP8X4),
                scales=plane[:, i, :, :].rearrange("p g n -> p (g n)"),
                in_=grouped_of[0][:, i, :, :, :].rearrange("p g n t -> p (g n t)"),
            )

        def quantise_pair(pair):
            codes = mx_pool.tile([P, PAIR, PASSES, P], U32, name="codes", align_bytes=64)
            plane = mx_pool.tile([P, PAIR, PASSES, P], U8, name="plane", align_bytes=64)
            nc.vector.quantize_mx(
                out=codes[:].rearrange("p i g n -> p (i g n)").bitcast(FP8X4),
                scales=plane[:].rearrange("p i g n -> p (i g n)"),
                in_=grouped_of[pair][:].rearrange("p i g n t -> p (i g n t)"),
            )
            codes_of[pair] = (codes, plane)
            if pair + SORT_AHEAD < PAIRS:
                sort_second(pair + SORT_AHEAD, codes)

        def multiply(j, projections=(0, 1)):
            pair, i = divmod(j, PAIR)
            codes, plane = codes_of[pair]
            acc_of.setdefault(j, [])
            for w in projections:
                acc = sum_banks.tile([P, E], F32, name="acc", tag="sums")
                for g in range(PASSES):
                    nc.tensor.matmul_mx(
                        out=acc[:],
                        lhsT=codes[:, i, g, :].bitcast(FP8X4),
                        lhsT_scale=plane[:, i, g, :],
                        rhs=w_words[:, w, g, :].bitcast(FP8X4),
                        rhs_scale=w_planes[:, w, g, :],
                        start=(g == 0),
                        stop=(g == PASSES - 1),
                    )
                acc_of[j].append(acc)
            if 0 in projections:
                sums_of[j] = stats.tile([P, 2 * HEADS], F32, name="sums")

        def head_square_sum(j, c):
            w, h = divmod(c, HEADS)
            squares = scrap.tile([P, DH], BF16, name="squares")
            nc.scalar.activation(
                out=squares[:],
                in_=acc_of[j][w][:, DH * h : DH * (h + 1)],
                func=ACT.Square,
                accum_out=sums_of[j][:, c : c + 1],
            )

        def reciprocal_root(j):
            rstd_of[j] = stats.tile([P, 2 * HEADS], F32, name="rstd")
            nc.scalar.activation(
                out=rstd_of[j][:],
                in_=sums_of[j][:],
                func=ACT.Abs_reciprocal_sqrt,
                bias=eps[:],
                scale=1.0 / DH,
            )

        def normalise(j, w):
            start, size = group_of[j]
            place = j - start
            if place == 0:
                pool = result if size == STORE else result_end
                out_of[(start, w)] = pool.tile([P, HEADS, size, DH], F32, name="normed%d" % w)
            normed = out_of[(start, w)]
            if (j, w) == (TILES - 1, 1):
                for h in range(HEADS):
                    nc.scalar.activation(
                        out=normed[:, h, place, :],
                        in_=acc_of[j][w][:, DH * h : DH * (h + 1)],
                        func=ACT.Copy,
                        scale=rstd_of[j][:, HEADS * w + h : HEADS * w + h + 1],
                    )
            else:
                nc.vector.tensor_tensor(
                    out=normed[:, :, place, :],
                    in0=acc_of[j][w][:].rearrange("p (h d) -> p h d", h=HEADS),
                    in1=rstd_of[j][:, HEADS * w : HEADS * (w + 1)].unsqueeze(2).to_broadcast([P, HEADS, DH]),
                    op=ALU.mult,
                )
            if place == size - 1:
                for s in range(HALVES):
                    token = TILES * s + start
                    nc.sync.dma_start(
                        out=outs[w][:, :, token : token + size, :].rearrange("b h j d -> b h (j d)"),
                        in_=normed[s:P:HALVES, :, :, :].rearrange("p h j d -> p h (j d)"),
                    )

        keep_warm(3)
        start_transpose(0)
        start_transpose(1)
        keep_warm(2)
        start_quantise(0)
        start_quantise(1)
        multiply(0, projections=(0,))
        multiply(1, projections=(0,))
        transpose_pair(1)
        copy_out(1, 0)
        copy_out(1, 1)
        multiply(0, projections=(1,))
        multiply(1, projections=(1,))
        for c in range(HEADS):
            head_square_sum(0, c)
        for c in range(HEADS):
            head_square_sum(1, c)
        for c in range(HEADS, 2 * HEADS):
            head_square_sum(0, c)
        head_square_sum(1, HEADS)
        reciprocal_root(0)
        for c in range(HEADS + 1, 2 * HEADS):
            head_square_sum(1, c)
        quantise_pair(1)
        normalise(0, 0)
        normalise(0, 1)
        for pair in range(1, PAIRS + 1):
            first, second = PAIR * pair, PAIR * pair + 1
            coming = pair + AHEAD
            if coming < PAIRS:
                transpose_pair(coming)
                copy_out(coming, 0)
                copy_out(coming, 1)
            if pair >= 1:
                reciprocal_root(first - 1)
            if pair < PAIRS:
                multiply(first)
                multiply(second)
                for c in range(2 * HEADS):
                    head_square_sum(first, c)
                head_square_sum(second, 0)
                reciprocal_root(first)
                for c in range(1, 2 * HEADS):
                    head_square_sum(second, c)
            if pair >= 1:
                normalise(first - 1, 0)
            if coming < PAIRS:
                quantise_pair(coming)
            if pair >= 1:
                normalise(first - 1, 1)
            if pair < PAIRS:
                normalise(first, 0)
                normalise(first, 1)
